import numpy as np
import ml_dtypes

BF16 = ml_dtypes.bfloat16


def bf(x):
    return np.asarray(x, np.float32).astype(BF16)


def f32(x):
    return np.asarray(x, np.float32)


def f64(x):
    return np.asarray(x).astype(np.float64)


def striped(idx):
    return np.tile(idx.reshape(-1, 16).T, (8, 1))


M, H, P, C, S, N = 3, 2, 128, 768, 512, 1024
FACTOR = 1.0 / np.sqrt(M)


def setup_inputs():
    return {"values": f32(np.random.standard_normal((C, S))), "grads_x": f32(np.random.standard_normal((C, N))), "grads_y": f32(np.random.standard_normal((C, N))), "grads_z": f32(np.random.standard_normal((C, N))), "offs": striped(np.random.permutation(np.tile(np.arange(S), 2))[:N])}


def reference(values, grads_x, grads_y, grads_z, offs):
    idx = offs[:16].T.reshape(-1)
    v = f64(values)[:, idx].reshape(M, H, P, N)
    rows = []
    for d in (grads_x, grads_y, grads_z):
        dsw = f64(d).reshape(M, H, P, N)[:, ::-1]
        rows.append(FACTOR * (v * dsw).sum(axis=(0, 1)))
    return np.concatenate(rows, axis=0)

@@ -1,0 +1,68 @@
+import math
+
+import concourse.mybir as mybir
+from concourse.masks import make_identity
+
+F32 = mybir.dt.float32
+U16 = mybir.dt.uint16
+MULT = mybir.AluOpType.mult
+COPY = mybir.ActivationFunctionType.Copy
+
+P = 128
+BLOCKS = 6
+DIRECTIONS = 3
+ATOMS = 512
+SAMPLES = 1024
+PIECE = 512
+PIECES = SAMPLES // PIECE
+FACTOR = 1.0 / math.sqrt(3.0)
+
+FLOPS = 2 * DIRECTIONS * BLOCKS * P * SAMPLES
+
+
+def tile_powerspectrum_kernel(tc, values, grads_x, grads_y, grads_z, offs, out):
+    nc = tc.nc
+    value_blocks = values.rearrange("(k p) s -> k p s", p=P)
+    grad_blocks = [g.rearrange("(k p) n -> k p n", p=P) for g in (grads_x, grads_y, grads_z)]
+    out_blocks = out.rearrange("(t p) n -> t p n", p=P)
+
+    with (
+        tc.tile_pool(name="held", bufs=1) as held,
+        tc.tile_pool(name="ring", bufs=6) as ring,
+        tc.psum_pool(name="sums", bufs=1) as sums,
+    ):
+        offsets = held.tile([P, SAMPLES // 16], U16, name="offsets")
+        nc.sync.dma_start(offsets[:], offs)
+
+        identity = held.tile([P, P], F32, name="identity")
+        make_identity(nc, identity[:])
+
+        banks = [
+            [sums.tile([P, PIECE], F32, name=f"bank{t}_{c}") for c in range(PIECES)]
+            for t in range(DIRECTIONS)
+        ]
+
+        for k in range(BLOCKS):
+            partner = k ^ 1
+            window = held.tile([P, ATOMS], F32, name=f"window{k}")
+            nc.sync.dma_start(window[:], value_blocks[k])
+            for t in range(DIRECTIONS):
+                grad = held.tile([P, SAMPLES], F32, name=f"grad{t}_{partner}")
+                nc.sync.dma_start(grad[:], grad_blocks[t][partner])
+                for c in range(PIECES):
+                    product = ring.tile([P, PIECE], F32, name="product")
+                    nc.vector.tensor_tensor(
+                        product[:],
+                        window[:].indirect(offsets[:, c * (PIECE // 16) : (c + 1) * (PIECE // 16)]),
+                        grad[:, c * PIECE : (c + 1) * PIECE],
+                        MULT,
+                    )
+                    nc.tensor.matmul(
+                        banks[t][c][:], identity[:], product[:], start=(k == 0), stop=(k == BLOCKS - 1)
+                    )
+
+        for t in range(DIRECTIONS):
+            for c in range(PIECES):
+                scaled = held.tile([P, PIECE], F32, name=f"scaled{t}_{c}")
+                nc.scalar.activation(scaled[:], banks[t][c][:], COPY, scale=FACTOR)
+                nc.scalar.dma_start(out_blocks[t][:, c * PIECE : (c + 1) * PIECE], scaled[:])

@@ -47,14 +47,14 @@ def tile_powerspectrum_kernel(tc, values, grads_x, grads_y, grads_z, offs, out):
             window = held.tile([P, ATOMS], F32, name=f"window{k}")
             nc.sync.dma_start(window[:], value_blocks[k])
             for t in range(DIRECTIONS):
-                grad = held.tile([P, SAMPLES], F32, name=f"grad{t}_{partner}")
-                nc.sync.dma_start(grad[:], grad_blocks[t][partner])
                 for c in range(PIECES):
+                    grad = held.tile([P, PIECE], F32, name=f"grad{t}_{partner}_{c}")
+                    nc.sync.dma_start(grad[:], grad_blocks[t][partner][:, c * PIECE : (c + 1) * PIECE])
                     product = ring.tile([P, PIECE], F32, name="product")
                     nc.vector.tensor_tensor(
                         product[:],
                         window[:].indirect(offsets[:, c * (PIECE // 16) : (c + 1) * (PIECE // 16)]),
-                        grad[:, c * PIECE : (c + 1) * PIECE],
+                        grad[:],
                         MULT,
                     )
                     nc.tensor.matmul(

@@ -6,6 +6,7 @@ from concourse.masks import make_identity
 F32 = mybir.dt.float32
 U16 = mybir.dt.uint16
 MULT = mybir.AluOpType.mult
+ADD = mybir.AluOpType.add
 COPY = mybir.ActivationFunctionType.Copy
 
 P = 128
@@ -37,8 +38,13 @@ def tile_powerspectrum_kernel(tc, values, grads_x, grads_y, grads_z, offs, out):
         identity = held.tile([P, P], F32, name="identity")
         make_identity(nc, identity[:])
 
-        banks = [
-            [sums.tile([P, PIECE], F32, name=f"bank{t}_{c}") for c in range(PIECES)]
+        totals = [
+            [
+                held.tile([P, PIECE], F32, name=f"total{t}_{c}")
+                if t == 0
+                else sums.tile([P, PIECE], F32, name=f"bank{t}_{c}")
+                for c in range(PIECES)
+            ]
             for t in range(DIRECTIONS)
         ]
 
@@ -50,19 +56,26 @@ def tile_powerspectrum_kernel(tc, values, grads_x, grads_y, grads_z, offs, out):
                 for c in range(PIECES):
                     grad = held.tile([P, PIECE], F32, name=f"grad{t}_{partner}_{c}")
                     nc.sync.dma_start(grad[:], grad_blocks[t][partner][:, c * PIECE : (c + 1) * PIECE])
-                    product = ring.tile([P, PIECE], F32, name="product")
+                    if t == 0 and k == 0:
+                        product = totals[t][c]
+                    else:
+                        product = ring.tile([P, PIECE], F32, name="product")
                     nc.vector.tensor_tensor(
                         product[:],
                         window[:].indirect(offsets[:, c * (PIECE // 16) : (c + 1) * (PIECE // 16)]),
                         grad[:],
                         MULT,
                     )
-                    nc.tensor.matmul(
-                        banks[t][c][:], identity[:], product[:], start=(k == 0), stop=(k == BLOCKS - 1)
-                    )
+                    if t == 0:
+                        if k > 0:
+                            nc.gpsimd.tensor_tensor(totals[t][c][:], totals[t][c][:], product[:], ADD)
+                    else:
+                        nc.tensor.matmul(
+                            totals[t][c][:], identity[:], product[:], start=(k == 0), stop=(k == BLOCKS - 1)
+                        )
 
         for t in range(DIRECTIONS):
             for c in range(PIECES):
                 scaled = held.tile([P, PIECE], F32, name=f"scaled{t}_{c}")
-                nc.scalar.activation(scaled[:], banks[t][c][:], COPY, scale=FACTOR)
+                nc.scalar.activation(scaled[:], totals[t][c][:], COPY, scale=FACTOR)
                 nc.scalar.dma_start(out_blocks[t][:, c * PIECE : (c + 1) * PIECE], scaled[:])

@@ -6,7 +6,6 @@ from concourse.masks import make_identity
 F32 = mybir.dt.float32
 U16 = mybir.dt.uint16
 MULT = mybir.AluOpType.mult
-ADD = mybir.AluOpType.add
 COPY = mybir.ActivationFunctionType.Copy
 
 P = 128
@@ -16,6 +15,8 @@ ATOMS = 512
 SAMPLES = 1024
 PIECE = 512
 PIECES = SAMPLES // PIECE
+WHOLE = [(0, PIECE)]
+LAST_CUTS = [(0, 256), (256, 128), (384, 128)]
 FACTOR = 1.0 / math.sqrt(3.0)
 
 FLOPS = 2 * DIRECTIONS * BLOCKS * P * SAMPLES
@@ -38,11 +39,11 @@ def tile_powerspectrum_kernel(tc, values, grads_x, grads_y, grads_z, offs, out):
         identity = held.tile([P, P], F32, name="identity")
         make_identity(nc, identity[:])
 
-        totals = [
+        cuts = [[WHOLE for c in range(PIECES)] for t in range(DIRECTIONS)]
+        cuts[DIRECTIONS - 1][PIECES - 1] = LAST_CUTS
+        banks = [
             [
-                held.tile([P, PIECE], F32, name=f"total{t}_{c}")
-                if t == 0
-                else sums.tile([P, PIECE], F32, name=f"bank{t}_{c}")
+                [sums.tile([P, width], F32, name=f"bank{t}_{c}_{first}") for first, width in cuts[t][c]]
                 for c in range(PIECES)
             ]
             for t in range(DIRECTIONS)
@@ -56,26 +57,28 @@ def tile_powerspectrum_kernel(tc, values, grads_x, grads_y, grads_z, offs, out):
                 for c in range(PIECES):
                     grad = held.tile([P, PIECE], F32, name=f"grad{t}_{partner}_{c}")
                     nc.sync.dma_start(grad[:], grad_blocks[t][partner][:, c * PIECE : (c + 1) * PIECE])
-                    if t == 0 and k == 0:
-                        product = totals[t][c]
-                    else:
-                        product = ring.tile([P, PIECE], F32, name="product")
-                    nc.vector.tensor_tensor(
-                        product[:],
-                        window[:].indirect(offsets[:, c * (PIECE // 16) : (c + 1) * (PIECE // 16)]),
-                        grad[:],
-                        MULT,
-                    )
-                    if t == 0:
-                        if k > 0:
-                            nc.gpsimd.tensor_tensor(totals[t][c][:], totals[t][c][:], product[:], ADD)
-                    else:
+                    product = ring.tile([P, PIECE], F32, name="product")
+                    for first, width in cuts[t][c] if k == BLOCKS - 1 else WHOLE:
+                        entry = c * PIECE + first
+                        nc.vector.tensor_tensor(
+                            product[:, first : first + width],
+                            window[:].indirect(offsets[:, entry // 16 : (entry + width) // 16]),
+                            grad[:, first : first + width],
+                            MULT,
+                        )
+                    for (first, width), bank in zip(cuts[t][c], banks[t][c]):
                         nc.tensor.matmul(
-                            totals[t][c][:], identity[:], product[:], start=(k == 0), stop=(k == BLOCKS - 1)
+                            bank[:],
+                            identity[:],
+                            product[:, first : first + width],
+                            start=(k == 0),
+                            stop=(k == BLOCKS - 1),
                         )
 
         for t in range(DIRECTIONS):
             for c in range(PIECES):
-                scaled = held.tile([P, PIECE], F32, name=f"scaled{t}_{c}")
-                nc.scalar.activation(scaled[:], totals[t][c][:], COPY, scale=FACTOR)
-                nc.scalar.dma_start(out_blocks[t][:, c * PIECE : (c + 1) * PIECE], scaled[:])
+                for (first, width), bank in zip(cuts[t][c], banks[t][c]):
+                    column = c * PIECE + first
+                    scaled = held.tile([P, width], F32, name=f"scaled{t}_{column}")
+                    nc.scalar.activation(scaled[:], bank[:], COPY, scale=FACTOR)
+                    nc.scalar.dma_start(out_blocks[t][:, column : column + width], scaled[:])

@@ -6,6 +6,7 @@ from concourse.masks import make_identity
 F32 = mybir.dt.float32
 U16 = mybir.dt.uint16
 MULT = mybir.AluOpType.mult
+ADD = mybir.AluOpType.add
 COPY = mybir.ActivationFunctionType.Copy
 
 P = 128
@@ -15,8 +16,7 @@ ATOMS = 512
 SAMPLES = 1024
 PIECE = 512
 PIECES = SAMPLES // PIECE
-WHOLE = [(0, PIECE)]
-LAST_CUTS = [(0, 256), (256, 128), (384, 128)]
+QUARTER = PIECE // 4
 FACTOR = 1.0 / math.sqrt(3.0)
 
 FLOPS = 2 * DIRECTIONS * BLOCKS * P * SAMPLES
@@ -27,6 +27,9 @@ def tile_powerspectrum_kernel(tc, values, grads_x, grads_y, grads_z, offs, out):
     value_blocks = values.rearrange("(k p) s -> k p s", p=P)
     grad_blocks = [g.rearrange("(k p) n -> k p n", p=P) for g in (grads_x, grads_y, grads_z)]
     out_blocks = out.rearrange("(t p) n -> t p n", p=P)
+    last_block = BLOCKS - 1
+    first_piece = (0, 0)
+    last_piece = (DIRECTIONS - 1, PIECES - 1)
 
     with (
         tc.tile_pool(name="held", bufs=1) as held,
@@ -39,46 +42,63 @@ def tile_powerspectrum_kernel(tc, values, grads_x, grads_y, grads_z, offs, out):
         identity = held.tile([P, P], F32, name="identity")
         make_identity(nc, identity[:])
 
-        cuts = [[WHOLE for c in range(PIECES)] for t in range(DIRECTIONS)]
-        cuts[DIRECTIONS - 1][PIECES - 1] = LAST_CUTS
-        banks = [
-            [
-                [sums.tile([P, width], F32, name=f"bank{t}_{c}_{first}") for first, width in cuts[t][c]]
-                for c in range(PIECES)
-            ]
-            for t in range(DIRECTIONS)
-        ]
+        cuts = {(t, c): [(0, PIECE)] for t in range(DIRECTIONS) for c in range(PIECES)}
+        cuts[first_piece] = [(0, QUARTER), (QUARTER, PIECE - QUARTER)]
+        cuts[last_piece] = [(0, QUARTER), (QUARTER, PIECE - QUARTER)]
+        banks = {
+            (t, c, first): sums.tile([P, width], F32, name=f"bank{t}_{c}_{first}")
+            for (t, c), piece_cuts in cuts.items()
+            for first, width in piece_cuts
+        }
+        closed_by_vector = (DIRECTIONS - 1, PIECES - 1, QUARTER)
+
+        def scale_bank(t, c, first, width):
+            scaled = held.tile([P, width], F32, name=f"scaled{t}_{c}_{first}")
+            nc.scalar.activation(scaled[:], banks[t, c, first][:], COPY, scale=FACTOR)
+            return scaled
 
         for k in range(BLOCKS):
             partner = k ^ 1
             window = held.tile([P, ATOMS], F32, name=f"window{k}")
             nc.sync.dma_start(window[:], value_blocks[k])
-            for t in range(DIRECTIONS):
-                for c in range(PIECES):
-                    grad = held.tile([P, PIECE], F32, name=f"grad{t}_{partner}_{c}")
-                    nc.sync.dma_start(grad[:], grad_blocks[t][partner][:, c * PIECE : (c + 1) * PIECE])
-                    product = ring.tile([P, PIECE], F32, name="product")
-                    for first, width in cuts[t][c] if k == BLOCKS - 1 else WHOLE:
-                        entry = c * PIECE + first
-                        nc.vector.tensor_tensor(
-                            product[:, first : first + width],
-                            window[:].indirect(offsets[:, entry // 16 : (entry + width) // 16]),
-                            grad[:, first : first + width],
-                            MULT,
-                        )
-                    for (first, width), bank in zip(cuts[t][c], banks[t][c]):
+            for t, c in cuts:
+                grad = held.tile([P, PIECE], F32, name=f"grad{t}_{partner}_{c}")
+                for first, width in cuts[t, c] if k == 0 else [(0, PIECE)]:
+                    nc.sync.dma_start(
+                        grad[:, first : first + width],
+                        grad_blocks[t][partner][:, c * PIECE + first : c * PIECE + first + width],
+                    )
+                product = ring.tile([P, PIECE], F32, name="product")
+                for first, width in cuts[t, c] if k in (0, last_block) else [(0, PIECE)]:
+                    entry = c * PIECE + first
+                    nc.vector.tensor_tensor(
+                        product[:, first : first + width],
+                        window[:].indirect(offsets[:, entry // 16 : (entry + width) // 16]),
+                        grad[:, first : first + width],
+                        MULT,
+                    )
+                for first, width in cuts[t, c]:
+                    columns = slice(first, first + width)
+                    if (t, c, first) != closed_by_vector:
                         nc.tensor.matmul(
-                            bank[:],
-                            identity[:],
-                            product[:, first : first + width],
-                            start=(k == 0),
-                            stop=(k == BLOCKS - 1),
+                            banks[t, c, first][:], identity[:], product[:, columns],
+                            start=(k == 0), stop=(k == last_block),
                         )
+                    elif k < last_block:
+                        nc.tensor.matmul(
+                            banks[t, c, first][:], identity[:], product[:, columns],
+                            start=(k == 0), stop=(k == last_block - 1),
+                        )
+                        if k == last_block - 1:
+                            five = scale_bank(t, c, first, width)
+                    else:
+                        closed = held.tile([P, width], F32, name="closed")
+                        nc.vector.scalar_tensor_tensor(closed[:], product[:, columns], FACTOR, five[:], MULT, ADD)
+                        nc.sync.dma_start(out_blocks[t][:, c * PIECE + first : c * PIECE + first + width], closed[:])
 
-        for t in range(DIRECTIONS):
-            for c in range(PIECES):
-                for (first, width), bank in zip(cuts[t][c], banks[t][c]):
+        for (t, c), piece_cuts in cuts.items():
+            for first, width in piece_cuts:
+                if (t, c, first) != closed_by_vector:
+                    scaled = scale_bank(t, c, first, width)
                     column = c * PIECE + first
-                    scaled = held.tile([P, width], F32, name=f"scaled{t}_{column}")
-                    nc.scalar.activation(scaled[:], bank[:], COPY, scale=FACTOR)
                     nc.scalar.dma_start(out_blocks[t][:, column : column + width], scaled[:])

@@ -16,8 +16,12 @@ ATOMS = 512
 SAMPLES = 1024
 PIECE = 512
 PIECES = SAMPLES // PIECE
-QUARTER = PIECE // 4
 FACTOR = 1.0 / math.sqrt(3.0)
+
+WHOLE = [(0, PIECE)]
+HALVES = [(0, PIECE // 2), (PIECE // 2, PIECE // 2)]
+SHORT_LONG = [(0, PIECE // 4), (PIECE // 4, PIECE - PIECE // 4)]
+SHORT_TWO = [(0, PIECE // 4), (PIECE // 4, 3 * PIECE // 8), (5 * PIECE // 8, 3 * PIECE // 8)]
 
 FLOPS = 2 * DIRECTIONS * BLOCKS * P * SAMPLES
 
@@ -27,9 +31,8 @@ def tile_powerspectrum_kernel(tc, values, grads_x, grads_y, grads_z, offs, out):
     value_blocks = values.rearrange("(k p) s -> k p s", p=P)
     grad_blocks = [g.rearrange("(k p) n -> k p n", p=P) for g in (grads_x, grads_y, grads_z)]
     out_blocks = out.rearrange("(t p) n -> t p n", p=P)
+    pieces = [(t, c) for t in range(DIRECTIONS) for c in range(PIECES)]
     last_block = BLOCKS - 1
-    first_piece = (0, 0)
-    last_piece = (DIRECTIONS - 1, PIECES - 1)
 
     with (
         tc.tile_pool(name="held", bufs=1) as held,
@@ -42,15 +45,17 @@ def tile_powerspectrum_kernel(tc, values, grads_x, grads_y, grads_z, offs, out):
         identity = held.tile([P, P], F32, name="identity")
         make_identity(nc, identity[:])
 
-        cuts = {(t, c): [(0, PIECE)] for t in range(DIRECTIONS) for c in range(PIECES)}
-        cuts[first_piece] = [(0, QUARTER), (QUARTER, PIECE - QUARTER)]
-        cuts[last_piece] = [(0, QUARTER), (QUARTER, PIECE - QUARTER)]
+        bank_cuts = {piece: WHOLE for piece in pieces}
+        bank_cuts[pieces[-2]] = HALVES
+        bank_cuts[pieces[-1]] = SHORT_LONG
+        closed_by_vector = pieces[-1] + (SHORT_LONG[-1][0],)
+        last_steps = dict(bank_cuts)
+        last_steps[pieces[-1]] = SHORT_TWO
         banks = {
             (t, c, first): sums.tile([P, width], F32, name=f"bank{t}_{c}_{first}")
-            for (t, c), piece_cuts in cuts.items()
-            for first, width in piece_cuts
+            for t, c in pieces
+            for first, width in bank_cuts[t, c]
         }
-        closed_by_vector = (DIRECTIONS - 1, PIECES - 1, QUARTER)
 
         def scale_bank(t, c, first, width):
             scaled = held.tile([P, width], F32, name=f"scaled{t}_{c}_{first}")
@@ -61,15 +66,16 @@ def tile_powerspectrum_kernel(tc, values, grads_x, grads_y, grads_z, offs, out):
             partner = k ^ 1
             window = held.tile([P, ATOMS], F32, name=f"window{k}")
             nc.sync.dma_start(window[:], value_blocks[k])
-            for t, c in cuts:
+            for t, c in pieces:
+                very_first = k == 0 and (t, c) == pieces[0]
                 grad = held.tile([P, PIECE], F32, name=f"grad{t}_{partner}_{c}")
-                for first, width in cuts[t, c] if k == 0 else [(0, PIECE)]:
+                for first, width in SHORT_LONG if very_first else WHOLE:
                     nc.sync.dma_start(
                         grad[:, first : first + width],
                         grad_blocks[t][partner][:, c * PIECE + first : c * PIECE + first + width],
                     )
                 product = ring.tile([P, PIECE], F32, name="product")
-                for first, width in cuts[t, c] if k in (0, last_block) else [(0, PIECE)]:
+                for first, width in SHORT_LONG if very_first else last_steps[t, c] if k == last_block else WHOLE:
                     entry = c * PIECE + first
                     nc.vector.tensor_tensor(
                         product[:, first : first + width],
@@ -77,7 +83,7 @@ def tile_powerspectrum_kernel(tc, values, grads_x, grads_y, grads_z, offs, out):
                         grad[:, first : first + width],
                         MULT,
                     )
-                for first, width in cuts[t, c]:
+                for first, width in bank_cuts[t, c]:
                     columns = slice(first, first + width)
                     if (t, c, first) != closed_by_vector:
                         nc.tensor.matmul(
@@ -92,12 +98,17 @@ def tile_powerspectrum_kernel(tc, values, grads_x, grads_y, grads_z, offs, out):
                         if k == last_block - 1:
                             five = scale_bank(t, c, first, width)
                     else:
-                        closed = held.tile([P, width], F32, name="closed")
-                        nc.vector.scalar_tensor_tensor(closed[:], product[:, columns], FACTOR, five[:], MULT, ADD)
-                        nc.sync.dma_start(out_blocks[t][:, c * PIECE + first : c * PIECE + first + width], closed[:])
+                        closed = held.tile([P, PIECE], F32, name="closed")
+                        for step_first, step_width in SHORT_TWO[1:]:
+                            step = slice(step_first, step_first + step_width)
+                            nc.vector.scalar_tensor_tensor(
+                                closed[:, step], product[:, step], FACTOR,
+                                five[:, step_first - first : step_first - first + step_width], MULT, ADD,
+                            )
+                        nc.sync.dma_start(out_blocks[t][:, c * PIECE + first : c * PIECE + first + width], closed[:, columns])
 
-        for (t, c), piece_cuts in cuts.items():
-            for first, width in piece_cuts:
+        for t, c in pieces:
+            for first, width in bank_cuts[t, c]:
                 if (t, c, first) != closed_by_vector:
                     scaled = scale_bank(t, c, first, width)
                     column = c * PIECE + first

@@ -21,7 +21,6 @@ FACTOR = 1.0 / math.sqrt(3.0)
 WHOLE = [(0, PIECE)]
 HALVES = [(0, PIECE // 2), (PIECE // 2, PIECE // 2)]
 SHORT_LONG = [(0, PIECE // 4), (PIECE // 4, PIECE - PIECE // 4)]
-SHORT_TWO = [(0, PIECE // 4), (PIECE // 4, 3 * PIECE // 8), (5 * PIECE // 8, 3 * PIECE // 8)]
 
 FLOPS = 2 * DIRECTIONS * BLOCKS * P * SAMPLES
 
@@ -46,11 +45,11 @@ def tile_powerspectrum_kernel(tc, values, grads_x, grads_y, grads_z, offs, out):
         make_identity(nc, identity[:])
 
         bank_cuts = {piece: WHOLE for piece in pieces}
+        bank_cuts[pieces[-3]] = HALVES
         bank_cuts[pieces[-2]] = HALVES
-        bank_cuts[pieces[-1]] = SHORT_LONG
-        closed_by_vector = pieces[-1] + (SHORT_LONG[-1][0],)
+        closed_by_vector = pieces[-1] + (0,)
         last_steps = dict(bank_cuts)
-        last_steps[pieces[-1]] = SHORT_TWO
+        last_steps[pieces[-1]] = HALVES
         banks = {
             (t, c, first): sums.tile([P, width], F32, name=f"bank{t}_{c}_{first}")
             for t, c in pieces
@@ -99,7 +98,7 @@ def tile_powerspectrum_kernel(tc, values, grads_x, grads_y, grads_z, offs, out):
                             five = scale_bank(t, c, first, width)
                     else:
                         closed = held.tile([P, PIECE], F32, name="closed")
-                        for step_first, step_width in SHORT_TWO[1:]:
+                        for step_first, step_width in HALVES:
                             step = slice(step_first, step_first + step_width)
                             nc.vector.scalar_tensor_tensor(
                                 closed[:, step], product[:, step], FACTOR,

@@ -21,6 +21,7 @@ FACTOR = 1.0 / math.sqrt(3.0)
 WHOLE = [(0, PIECE)]
 HALVES = [(0, PIECE // 2), (PIECE // 2, PIECE // 2)]
 SHORT_LONG = [(0, PIECE // 4), (PIECE // 4, PIECE - PIECE // 4)]
+QUARTERS = [(q * PIECE // 4, PIECE // 4) for q in range(4)]
 
 FLOPS = 2 * DIRECTIONS * BLOCKS * P * SAMPLES
 
@@ -64,7 +65,8 @@ def tile_powerspectrum_kernel(tc, values, grads_x, grads_y, grads_z, offs, out):
         for k in range(BLOCKS):
             partner = k ^ 1
             window = held.tile([P, ATOMS], F32, name=f"window{k}")
-            nc.sync.dma_start(window[:], value_blocks[k])
+            for first, width in QUARTERS if k == 0 else WHOLE:
+                nc.sync.dma_start(window[:, first : first + width], value_blocks[k][:, first : first + width])
             for t, c in pieces:
                 very_first = k == 0 and (t, c) == pieces[0]
                 grad = held.tile([P, PIECE], F32, name=f"grad{t}_{partner}_{c}")

@@ -40,7 +40,6 @@ def tile_powerspectrum_kernel(tc, values, grads_x, grads_y, grads_z, offs, out):
         tc.psum_pool(name="sums", bufs=1) as sums,
     ):
         offsets = held.tile([P, SAMPLES // 16], U16, name="offsets")
-        nc.sync.dma_start(offsets[:], offs)
 
         identity = held.tile([P, P], F32, name="identity")
         make_identity(nc, identity[:])
@@ -75,6 +74,8 @@ def tile_powerspectrum_kernel(tc, values, grads_x, grads_y, grads_z, offs, out):
                         grad[:, first : first + width],
                         grad_blocks[t][partner][:, c * PIECE + first : c * PIECE + first + width],
                     )
+                    if very_first and first == 0:
+                        nc.sync.dma_start(offsets[:], offs)
                 product = ring.tile([P, PIECE], F32, name="product")
                 for first, width in SHORT_LONG if very_first else last_steps[t, c] if k == last_block else WHOLE:
                     entry = c * PIECE + first

@@ -20,6 +20,7 @@ FACTOR = 1.0 / math.sqrt(3.0)
 
 WHOLE = [(0, PIECE)]
 HALVES = [(0, PIECE // 2), (PIECE // 2, PIECE // 2)]
+LONG_SHORT = [(0, 5 * PIECE // 8), (5 * PIECE // 8, 3 * PIECE // 8)]
 SHORT_LONG = [(0, PIECE // 4), (PIECE // 4, PIECE - PIECE // 4)]
 QUARTERS = [(q * PIECE // 4, PIECE // 4) for q in range(4)]
 
@@ -46,7 +47,7 @@ def tile_powerspectrum_kernel(tc, values, grads_x, grads_y, grads_z, offs, out):
 
         bank_cuts = {piece: WHOLE for piece in pieces}
         bank_cuts[pieces[-3]] = HALVES
-        bank_cuts[pieces[-2]] = HALVES
+        bank_cuts[pieces[-2]] = LONG_SHORT
         closed_by_vector = pieces[-1] + (0,)
         last_steps = dict(bank_cuts)
         last_steps[pieces[-1]] = HALVES

import math

import concourse.mybir as mybir
from concourse.masks import make_identity

F32 = mybir.dt.float32
U16 = mybir.dt.uint16
MULT = mybir.AluOpType.mult
ADD = mybir.AluOpType.add
COPY = mybir.ActivationFunctionType.Copy

P = 128
BLOCKS = 6
DIRECTIONS = 3
ATOMS = 512
SAMPLES = 1024
PIECE = 512
PIECES = SAMPLES // PIECE
FACTOR = 1.0 / math.sqrt(3.0)

WHOLE = [(0, PIECE)]
HALVES = [(0, PIECE // 2), (PIECE // 2, PIECE // 2)]
LONG_SHORT = [(0, 5 * PIECE // 8), (5 * PIECE // 8, 3 * PIECE // 8)]
SHORT_LONG = [(0, PIECE // 4), (PIECE // 4, PIECE - PIECE // 4)]
QUARTERS = [(q * PIECE // 4, PIECE // 4) for q in range(4)]

FLOPS = 2 * DIRECTIONS * BLOCKS * P * SAMPLES


def tile_powerspectrum_kernel(tc, values, grads_x, grads_y, grads_z, offs, out):
    nc = tc.nc
    value_blocks = values.rearrange("(k p) s -> k p s", p=P)
    grad_blocks = [g.rearrange("(k p) n -> k p n", p=P) for g in (grads_x, grads_y, grads_z)]
    out_blocks = out.rearrange("(t p) n -> t p n", p=P)
    pieces = [(t, c) for t in range(DIRECTIONS) for c in range(PIECES)]
    last_block = BLOCKS - 1

    with (
        tc.tile_pool(name="held", bufs=1) as held,
        tc.tile_pool(name="ring", bufs=6) as ring,
        tc.psum_pool(name="sums", bufs=1) as sums,
    ):
        offsets = held.tile([P, SAMPLES // 16], U16, name="offsets")

        identity = held.tile([P, P], F32, name="identity")
        make_identity(nc, identity[:])

        bank_cuts = {piece: WHOLE for piece in pieces}
        bank_cuts[pieces[-3]] = HALVES
        bank_cuts[pieces[-2]] = LONG_SHORT
        closed_by_vector = pieces[-1] + (0,)
        last_steps = dict(bank_cuts)
        last_steps[pieces[-1]] = HALVES
        banks = {
            (t, c, first): sums.tile([P, width], F32, name=f"bank{t}_{c}_{first}")
            for t, c in pieces
            for first, width in bank_cuts[t, c]
        }

        def scale_bank(t, c, first, width):
            scaled = held.tile([P, width], F32, name=f"scaled{t}_{c}_{first}")
            nc.scalar.activation(scaled[:], banks[t, c, first][:], COPY, scale=FACTOR)
            return scaled

        for k in range(BLOCKS):
            partner = k ^ 1
            window = held.tile([P, ATOMS], F32, name=f"window{k}")
            for first, width in QUARTERS if k == 0 else WHOLE:
                nc.sync.dma_start(window[:, first : first + width], value_blocks[k][:, first : first + width])
            for t, c in pieces:
                very_first = k == 0 and (t, c) == pieces[0]
                grad = held.tile([P, PIECE], F32, name=f"grad{t}_{partner}_{c}")
                for first, width in SHORT_LONG if very_first else WHOLE:
                    nc.sync.dma_start(
                        grad[:, first : first + width],
                        grad_blocks[t][partner][:, c * PIECE + first : c * PIECE + first + width],
                    )
                    if very_first and first == 0:
                        nc.sync.dma_start(offsets[:], offs)
                product = ring.tile([P, PIECE], F32, name="product")
                for first, width in SHORT_LONG if very_first else last_steps[t, c] if k == last_block else WHOLE:
                    entry = c * PIECE + first
                    nc.vector.tensor_tensor(
                        product[:, first : first + width],
                        window[:].indirect(offsets[:, entry // 16 : (entry + width) // 16]),
                        grad[:, first : first + width],
                        MULT,
                    )
                for first, width in bank_cuts[t, c]:
                    columns = slice(first, first + width)
                    if (t, c, first) != closed_by_vector:
                        nc.tensor.matmul(
                            banks[t, c, first][:], identity[:], product[:, columns],
                            start=(k == 0), stop=(k == last_block),
                        )
                    elif k < last_block:
                        nc.tensor.matmul(
                            banks[t, c, first][:], identity[:], product[:, columns],
                            start=(k == 0), stop=(k == last_block - 1),
                        )
                        if k == last_block - 1:
                            five = scale_bank(t, c, first, width)
                    else:
                        closed = held.tile([P, PIECE], F32, name="closed")
                        for step_first, step_width in HALVES:
                            step = slice(step_first, step_first + step_width)
                            nc.vector.scalar_tensor_tensor(
                                closed[:, step], product[:, step], FACTOR,
                                five[:, step_first - first : step_first - first + step_width], MULT, ADD,
                            )
                        nc.sync.dma_start(out_blocks[t][:, c * PIECE + first : c * PIECE + first + width], closed[:, columns])

        for t, c in pieces:
            for first, width in bank_cuts[t, c]:
                if (t, c, first) != closed_by_vector:
                    scaled = scale_bank(t, c, first, width)
                    column = c * PIECE + first
                    nc.scalar.dma_start(out_blocks[t][:, column : column + width], scaled[:])
